import numpy as np
import ml_dtypes


def mxq(x, axis, fmt="e4m3"):
    dtype, down = {"e4m3": (ml_dtypes.float8_e4m3fn, 7), "e5m2": (ml_dtypes.float8_e5m2, 14)}[fmt]
    v = np.moveaxis(np.asarray(x, np.float32).astype(ml_dtypes.bfloat16).astype(np.float64), axis, -1)
    blocks = v.reshape(v.shape[:-1] + (-1, 32))
    amax = np.abs(blocks).max(-1, keepdims=True)
    byte = np.maximum(np.where(amax > 0, np.frexp(amax)[1] - 1 + 127, 0) - down, 1)
    scale = np.exp2(byte - 127.0)
    codes = (blocks / scale).astype(np.float32).astype(dtype).astype(np.float64)
    return np.moveaxis((codes * scale).reshape(v.shape), -1, axis)


WIDE = False


def mx_kscale(k):
    if not WIDE:
        return np.ones(k)
    levels = np.array([20, -20, 10, -10, 0])
    a = np.random.permutation(np.resize(levels, k // 512 * 4)).reshape(k // 512, 4)
    idx = np.arange(k)
    return np.exp2(a[idx // 512, idx % 128 // 32])


BF16 = ml_dtypes.bfloat16


def bf(x):
    return np.asarray(x, np.float32).astype(BF16)


def f64(x):
    return np.asarray(x).astype(np.float64)


B, N, F = 8, 512, 512


def setup_inputs():
    u = mx_kscale(F)
    regional_means = np.random.standard_normal((B, N, F)) * (4.0 / np.sqrt(N)) / u
    adj = np.random.uniform(0.0, 1.0, (B, N, N))
    g = np.random.standard_normal((B, N, F)) * np.exp2(np.random.randint(-12, 1, (B, N, 1))) * 8.0 * u
    return {"regional_means": bf(regional_means), "adj": bf(adj), "grad_out": bf(g)}


def reference(regional_means, adj, grad_out):
    n = adj.shape[-1]
    mask = 1.0 - np.eye(n)
    g = mxq(f64(grad_out), 2, "e5m2")
    r = mxq(f64(regional_means), 2, "e4m3")
    p = g @ r.transpose(0, 2, 1)
    return p * mask

@@ -1,0 +1,170 @@
+from contextlib import ExitStack
+
+import concourse.mybir as mybir
+from concourse.masks import make_identity
+
+FP32 = mybir.dt.float32
+BF16 = mybir.dt.bfloat16
+U32 = mybir.dt.uint32
+U8 = mybir.dt.uint8
+E4X4 = mybir.dt.float8_e4m3fn_x4
+E5X4 = mybir.dt.float8_e5m2_x4
+
+B = 8
+N = 512
+F = 512
+P = 128
+
+FLOPS = 2 * B * N * N * F
+BYTES = 2 * (B * N * F * 2) + B * N * N * 4
+
+
+def tile_gcn_kernel(tc, regional_means, adj, grad_out, out):
+    nc = tc.nc
+    with ExitStack() as ctx:
+        ctx.enter_context(tc.manual_schedule())
+        const = ctx.enter_context(tc.tile_pool(name="const", bufs=1))
+        inputs = ctx.enter_context(tc.tile_pool(name="inputs", bufs=1))
+        results = ctx.enter_context(tc.tile_pool(name="results", bufs=1))
+        grouped = ctx.enter_context(tc.tile_pool(name="grouped", bufs=6))
+        quant = ctx.enter_context(tc.tile_pool(name="quant", bufs=3))
+        psum_t = ctx.enter_context(tc.psum_pool(name="psum_t", bufs=4))
+        psum_o = ctx.enter_context(tc.psum_pool(name="psum_o", bufs=4))
+
+        r_words = []
+        g_words = []
+        for b in range(B):
+            r_t = inputs.tile([P, 2048], BF16, name="r_in%d" % b)
+            g_t = inputs.tile([P, 2048], BF16, name="g_in%d" % b)
+            r_src = regional_means[b].rearrange("(h p t) k -> p h t k", h=2, t=2)
+            g_src = grad_out[b].rearrange("(p m) k -> p m k", m=4)
+            r_dst = r_t[:].rearrange("p (h t k) -> p h t k", h=2, t=2)
+            g_dst = g_t[:].rearrange("p (m k) -> p m k", m=4)
+            if b == 0:
+                for h in range(2):
+                    nc.sync.dma_start(out=r_dst[:, h], in_=r_src[:, h])
+                for q in range(2):
+                    nc.sync.dma_start(
+                        out=g_dst[:, 2 * q : 2 * q + 2], in_=g_src[:, 2 * q : 2 * q + 2]
+                    )
+            else:
+                nc.sync.dma_start(out=r_dst, in_=r_src)
+                nc.sync.dma_start(out=g_dst, in_=g_src)
+            r_words.append(r_t[:].bitcast(FP32))
+            g_words.append(g_t[:].bitcast(FP32))
+
+        ident = const.tile([P, P], FP32, name="ident")
+        make_identity(nc, ident[:])
+        mask = const.tile([P, 4 * N], FP32, name="mask")
+        nc.vector.memset(mask[:], 1.0)
+        for m in range(4):
+            nc.gpsimd.affine_select(
+                out=mask[:, N * m : N * (m + 1)],
+                in_=mask[:, N * m : N * (m + 1)],
+                compare_op=mybir.AluOpType.not_equal,
+                fill=0.0,
+                base=m,
+                pattern=[[-1, N]],
+                channel_multiplier=4,
+            )
+
+        state = {}
+
+        def transposes(b, which):
+            words = r_words[b] if which == "r" else g_words[b]
+            tiles = []
+            for half in range(2):
+                bank = psum_t.tile([P, 512], FP32, name="bank")
+                for a in range(4):
+                    lo = 512 * half + 128 * a
+                    nc.tensor.transpose(
+                        bank[:, 128 * a : 128 * (a + 1)], words[:, lo : lo + 128], ident[:]
+                    )
+                grp = grouped.tile([P, 1024], BF16, name="grp", align_bytes=64)
+                dst = grp[:].bitcast(FP32)
+                if which == "r":
+                    nc.scalar.copy(
+                        out=dst.rearrange("p (c a) -> p c a", a=4),
+                        in_=bank[:].rearrange("p (a c) -> p c a", a=4),
+                    )
+                else:
+                    nc.scalar.copy(
+                        out=dst.rearrange("p (l c u) -> p l c u", l=2, u=2),
+                        in_=bank[:].rearrange("p (l u c) -> p l c u", l=2, u=2),
+                    )
+                tiles.append(grp)
+            state[(b, which, "grp")] = tiles
+
+        def quantise(b, which):
+            codes = quant.tile([P, 512], U32, name="codes_" + which, align_bytes=64)
+            scales = quant.tile([P, 512], U8, name="scales_" + which, align_bytes=64)
+            fmt = E4X4 if which == "r" else E5X4
+            for half in range(2):
+                cols = slice(256 * half, 256 * (half + 1))
+                nc.vector.quantize_mx(
+                    out=codes[:, cols].bitcast(fmt),
+                    scales=scales[:, cols],
+                    in_=state[(b, which, "grp")][half][:],
+                )
+            state[(b, which)] = (codes, scales)
+
+        def multiply(b, pair):
+            r_codes, r_scales = state[(b, "r")]
+            g_codes, g_scales = state[(b, "g")]
+            accs = []
+            for m in (2 * pair, 2 * pair + 1):
+                acc = psum_o.tile([P, N], FP32, name="acc")
+                cols = slice(P * m, P * (m + 1))
+                nc.tensor.matmul_mx(
+                    out=acc[:],
+                    lhsT=g_codes[:, cols].bitcast(E5X4),
+                    lhsT_scale=g_scales[:, cols],
+                    rhs=r_codes[:].bitcast(E4X4),
+                    rhs_scale=r_scales[:],
+                    start=True,
+                    stop=True,
+                )
+                accs.append(acc)
+            state[(b, "acc", pair)] = accs
+
+        def leave(b, pair):
+            if pair == 0:
+                state[(b, "res")] = results.tile([P, 4 * N], FP32, name="res%d" % b)
+            res = state[(b, "res")]
+            for i in range(2):
+                m = 2 * pair + i
+                cols = slice(N * m, N * (m + 1))
+                nc.vector.tensor_tensor(
+                    out=res[:, cols],
+                    in0=state[(b, "acc", pair)][i][:],
+                    in1=mask[:, cols],
+                    op=mybir.AluOpType.mult,
+                )
+
+        transposes(0, "r")
+        quantise(0, "r")
+        transposes(0, "g")
+        quantise(0, "g")
+        for b in range(B):
+            more = b + 1 < B
+            dst = out[b].rearrange("(p m) j -> p m j", m=4)
+            if more:
+                transposes(b + 1, "r")
+            multiply(b, 0)
+            if more:
+                quantise(b + 1, "r")
+            leave(b, 0)
+            if not more:
+                src = state[(b, "res")][:].rearrange("p (m j) -> p m j", m=4)
+                nc.sync.dma_start(out=dst[:, 0:2], in_=src[:, 0:2])
+            if more:
+                transposes(b + 1, "g")
+            multiply(b, 1)
+            if more:
+                quantise(b + 1, "g")
+            leave(b, 1)
+            src = state[(b, "res")][:].rearrange("p (m j) -> p m j", m=4)
+            if more:
+                nc.sync.dma_start(out=dst, in_=src)
+            else:
+                nc.sync.dma_start(out=dst[:, 2:4], in_=src[:, 2:4])

@@ -134,12 +134,24 @@ def tile_gcn_kernel(tc, regional_means, adj, grad_out, out):
             for i in range(2):
                 m = 2 * pair + i
                 cols = slice(N * m, N * (m + 1))
-                nc.vector.tensor_tensor(
-                    out=res[:, cols],
-                    in0=state[(b, "acc", pair)][i][:],
-                    in1=mask[:, cols],
-                    op=mybir.AluOpType.mult,
-                )
+                if m == 1:
+                    nc.scalar.copy(out=res[:, cols], in_=state[(b, "acc", pair)][i][:])
+                    nc.gpsimd.affine_select(
+                        out=res[:, cols],
+                        in_=res[:, cols],
+                        compare_op=mybir.AluOpType.not_equal,
+                        fill=0.0,
+                        base=m,
+                        pattern=[[-1, N]],
+                        channel_multiplier=4,
+                    )
+                else:
+                    nc.vector.tensor_tensor(
+                        out=res[:, cols],
+                        in0=state[(b, "acc", pair)][i][:],
+                        in1=mask[:, cols],
+                        op=mybir.AluOpType.mult,
+                    )
 
         transposes(0, "r")
         quantise(0, "r")

@@ -26,7 +26,8 @@ def tile_gcn_kernel(tc, regional_means, adj, grad_out, out):
         const = ctx.enter_context(tc.tile_pool(name="const", bufs=1))
         inputs = ctx.enter_context(tc.tile_pool(name="inputs", bufs=1))
         results = ctx.enter_context(tc.tile_pool(name="results", bufs=1))
-        grouped = ctx.enter_context(tc.tile_pool(name="grouped", bufs=6))
+        grouped = ctx.enter_context(tc.tile_pool(name="grouped", bufs=4))
+        grouped_r = ctx.enter_context(tc.tile_pool(name="grouped_r", bufs=3))
         quant = ctx.enter_context(tc.tile_pool(name="quant", bufs=3))
         psum_t = ctx.enter_context(tc.psum_pool(name="psum_t", bufs=4))
         psum_o = ctx.enter_context(tc.psum_pool(name="psum_o", bufs=4))
@@ -36,13 +37,15 @@ def tile_gcn_kernel(tc, regional_means, adj, grad_out, out):
         for b in range(B):
             r_t = inputs.tile([P, 2048], BF16, name="r_in%d" % b)
             g_t = inputs.tile([P, 2048], BF16, name="g_in%d" % b)
-            r_src = regional_means[b].rearrange("(h p t) k -> p h t k", h=2, t=2)
+            r_src = regional_means[b].rearrange("(p m) k -> p m k", m=4)
             g_src = grad_out[b].rearrange("(p m) k -> p m k", m=4)
-            r_dst = r_t[:].rearrange("p (h t k) -> p h t k", h=2, t=2)
+            r_dst = r_t[:].rearrange("p (m k) -> p m k", m=4)
             g_dst = g_t[:].rearrange("p (m k) -> p m k", m=4)
             if b == 0:
-                for h in range(2):
-                    nc.sync.dma_start(out=r_dst[:, h], in_=r_src[:, h])
+                for q in range(2):
+                    nc.sync.dma_start(
+                        out=r_dst[:, 2 * q : 2 * q + 2], in_=r_src[:, 2 * q : 2 * q + 2]
+                    )
                 for q in range(2):
                     nc.sync.dma_start(
                         out=g_dst[:, 2 * q : 2 * q + 2], in_=g_src[:, 2 * q : 2 * q + 2]
@@ -73,6 +76,9 @@ def tile_gcn_kernel(tc, regional_means, adj, grad_out, out):
         def transposes(b, which):
             words = r_words[b] if which == "r" else g_words[b]
             tiles = []
+            if which == "r":
+                wide = grouped_r.tile([P, 2048], BF16, name="wide", align_bytes=64)
+                tiles.append(wide)
             for half in range(2):
                 bank = psum_t.tile([P, 512], FP32, name="bank")
                 for a in range(4):
@@ -80,26 +86,33 @@ def tile_gcn_kernel(tc, regional_means, adj, grad_out, out):
                     nc.tensor.transpose(
                         bank[:, 128 * a : 128 * (a + 1)], words[:, lo : lo + 128], ident[:]
                     )
-                grp = grouped.tile([P, 1024], BF16, name="grp", align_bytes=64)
-                dst = grp[:].bitcast(FP32)
                 if which == "r":
+                    dst = wide[:].bitcast(FP32).rearrange("p (c q a) -> p q c a", q=2, a=4)
                     nc.scalar.copy(
-                        out=dst.rearrange("p (c a) -> p c a", a=4),
+                        out=dst[:, half],
                         in_=bank[:].rearrange("p (a c) -> p c a", a=4),
                     )
                 else:
+                    grp = grouped.tile([P, 1024], BF16, name="grp", align_bytes=64)
+                    dst = grp[:].bitcast(FP32)
                     nc.scalar.copy(
                         out=dst.rearrange("p (l c u) -> p l c u", l=2, u=2),
                         in_=bank[:].rearrange("p (l u c) -> p l c u", l=2, u=2),
                     )
-                tiles.append(grp)
+                    tiles.append(grp)
             state[(b, which, "grp")] = tiles
 
         def quantise(b, which):
             codes = quant.tile([P, 512], U32, name="codes_" + which, align_bytes=64)
             scales = quant.tile([P, 512], U8, name="scales_" + which, align_bytes=64)
             fmt = E4X4 if which == "r" else E5X4
-            for half in range(2):
+            if which == "r":
+                nc.vector.quantize_mx(
+                    out=codes[:].bitcast(fmt),
+                    scales=scales[:],
+                    in_=state[(b, which, "grp")][0][:],
+                )
+            for half in range(2 if which == "g" else 0):
                 cols = slice(256 * half, 256 * (half + 1))
                 nc.vector.quantize_mx(
                     out=codes[:, cols].bitcast(fmt),

@@ -41,18 +41,8 @@ def tile_gcn_kernel(tc, regional_means, adj, grad_out, out):
             g_src = grad_out[b].rearrange("(p m) k -> p m k", m=4)
             r_dst = r_t[:].rearrange("p (m k) -> p m k", m=4)
             g_dst = g_t[:].rearrange("p (m k) -> p m k", m=4)
-            if b == 0:
-                for q in range(2):
-                    nc.sync.dma_start(
-                        out=r_dst[:, 2 * q : 2 * q + 2], in_=r_src[:, 2 * q : 2 * q + 2]
-                    )
-                for q in range(2):
-                    nc.sync.dma_start(
-                        out=g_dst[:, 2 * q : 2 * q + 2], in_=g_src[:, 2 * q : 2 * q + 2]
-                    )
-            else:
-                nc.sync.dma_start(out=r_dst, in_=r_src)
-                nc.sync.dma_start(out=g_dst, in_=g_src)
+            nc.sync.dma_start(out=r_dst, in_=r_src)
+            nc.sync.dma_start(out=g_dst, in_=g_src)
             r_words.append(r_t[:].bitcast(FP32))
             g_words.append(g_t[:].bitcast(FP32))
 
@@ -179,9 +169,6 @@ def tile_gcn_kernel(tc, regional_means, adj, grad_out, out):
             if more:
                 quantise(b + 1, "r")
             leave(b, 0)
-            if not more:
-                src = state[(b, "res")][:].rearrange("p (m j) -> p m j", m=4)
-                nc.sync.dma_start(out=dst[:, 0:2], in_=src[:, 0:2])
             if more:
                 transposes(b + 1, "g")
             multiply(b, 1)
@@ -189,7 +176,4 @@ def tile_gcn_kernel(tc, regional_means, adj, grad_out, out):
                 quantise(b + 1, "g")
             leave(b, 1)
             src = state[(b, "res")][:].rearrange("p (m j) -> p m j", m=4)
-            if more:
-                nc.sync.dma_start(out=dst, in_=src)
-            else:
-                nc.sync.dma_start(out=dst[:, 2:4], in_=src[:, 2:4])
+            nc.sync.dma_start(out=dst, in_=src)

@@ -14,6 +14,7 @@ B = 8
 N = 512
 F = 512
 P = 128
+PAIRS = B // 2
 
 FLOPS = 2 * B * N * N * F
 BYTES = 2 * (B * N * F * 2) + B * N * N * 4
@@ -26,25 +27,18 @@ def tile_gcn_kernel(tc, regional_means, adj, grad_out, out):
         const = ctx.enter_context(tc.tile_pool(name="const", bufs=1))
         inputs = ctx.enter_context(tc.tile_pool(name="inputs", bufs=1))
         results = ctx.enter_context(tc.tile_pool(name="results", bufs=1))
-        grouped = ctx.enter_context(tc.tile_pool(name="grouped", bufs=4))
-        grouped_r = ctx.enter_context(tc.tile_pool(name="grouped_r", bufs=3))
-        quant = ctx.enter_context(tc.tile_pool(name="quant", bufs=3))
+        grouped = ctx.enter_context(tc.tile_pool(name="grouped", bufs=2))
+        quant = ctx.enter_context(tc.tile_pool(name="quant", bufs=4))
         psum_t = ctx.enter_context(tc.psum_pool(name="psum_t", bufs=4))
         psum_o = ctx.enter_context(tc.psum_pool(name="psum_o", bufs=4))
 
-        r_words = []
-        g_words = []
-        for b in range(B):
-            r_t = inputs.tile([P, 2048], BF16, name="r_in%d" % b)
-            g_t = inputs.tile([P, 2048], BF16, name="g_in%d" % b)
-            r_src = regional_means[b].rearrange("(p m) k -> p m k", m=4)
-            g_src = grad_out[b].rearrange("(p m) k -> p m k", m=4)
-            r_dst = r_t[:].rearrange("p (m k) -> p m k", m=4)
-            g_dst = g_t[:].rearrange("p (m k) -> p m k", m=4)
-            nc.sync.dma_start(out=r_dst, in_=r_src)
-            nc.sync.dma_start(out=g_dst, in_=g_src)
-            r_words.append(r_t[:].bitcast(FP32))
-            g_words.append(g_t[:].bitcast(FP32))
+        in_words = {}
+        for pair in range(PAIRS):
+            for which, src_all in (("r", regional_means), ("g", grad_out)):
+                t = inputs.tile([P, 4096], BF16, name="%s_in%d" % (which, pair))
+                rows = src_all.flatten_outer_dims()[2 * N * pair : 2 * N * (pair + 1), :]
+                nc.sync.dma_start(out=t[:], in_=rows.rearrange("(p m) k -> p (m k)", m=8))
+                in_words[(pair, which)] = t[:].bitcast(FP32)
 
         ident = const.tile([P, P], FP32, name="ident")
         make_identity(nc, ident[:])
@@ -63,59 +57,65 @@ def tile_gcn_kernel(tc, regional_means, adj, grad_out, out):
 
         state = {}
 
-        def transposes(b, which):
-            words = r_words[b] if which == "r" else g_words[b]
-            tiles = []
-            if which == "r":
-                wide = grouped_r.tile([P, 2048], BF16, name="wide", align_bytes=64)
-                tiles.append(wide)
-            for half in range(2):
+        def transposes(pair, which, run):
+            words = in_words[(pair, which)]
+            if run == 0:
+                state[(pair, which, "wide")] = grouped.tile(
+                    [P, 4096], BF16, name="wide_" + which, align_bytes=64
+                )
+            wide_words = state[(pair, which, "wide")][:].bitcast(FP32)
+            for i in (2 * run, 2 * run + 1):
                 bank = psum_t.tile([P, 512], FP32, name="bank")
                 for a in range(4):
-                    lo = 512 * half + 128 * a
+                    if which == "r":
+                        lo = 512 * i + 128 * a
+                    else:
+                        lo = 256 * (i + 4 * (a // 2)) + 128 * (a % 2)
                     nc.tensor.transpose(
                         bank[:, 128 * a : 128 * (a + 1)], words[:, lo : lo + 128], ident[:]
                     )
                 if which == "r":
-                    dst = wide[:].bitcast(FP32).rearrange("p (c q a) -> p q c a", q=2, a=4)
-                    nc.scalar.copy(
-                        out=dst[:, half],
-                        in_=bank[:].rearrange("p (a c) -> p c a", a=4),
-                    )
+                    dst = wide_words.rearrange("p (h c i a) -> p i h c a", h=2, i=4, a=4)
                 else:
-                    grp = grouped.tile([P, 1024], BF16, name="grp", align_bytes=64)
-                    dst = grp[:].bitcast(FP32)
-                    nc.scalar.copy(
-                        out=dst.rearrange("p (l c u) -> p l c u", l=2, u=2),
-                        in_=bank[:].rearrange("p (l u c) -> p l c u", l=2, u=2),
-                    )
-                    tiles.append(grp)
-            state[(b, which, "grp")] = tiles
-
-        def quantise(b, which):
-            codes = quant.tile([P, 512], U32, name="codes_" + which, align_bytes=64)
-            scales = quant.tile([P, 512], U8, name="scales_" + which, align_bytes=64)
-            fmt = E4X4 if which == "r" else E5X4
-            if which == "r":
-                nc.vector.quantize_mx(
-                    out=codes[:].bitcast(fmt),
-                    scales=scales[:],
-                    in_=state[(b, which, "grp")][0][:],
+                    dst = wide_words.rearrange("p (h i c a) -> p i h c a", h=2, i=4, a=4)
+                nc.scalar.copy(
+                    out=dst[:, i],
+                    in_=bank[:].rearrange("p (a h c) -> p h c a", a=4, h=2),
                 )
-            for half in range(2 if which == "g" else 0):
-                cols = slice(256 * half, 256 * (half + 1))
-                nc.vector.quantize_mx(
-                    out=codes[:, cols].bitcast(fmt),
-                    scales=scales[:, cols],
-                    in_=state[(b, which, "grp")][half][:],
-                )
-            state[(b, which)] = (codes, scales)
 
-        def multiply(b, pair):
-            r_codes, r_scales = state[(b, "r")]
-            g_codes, g_scales = state[(b, "g")]
-            accs = []
-            for m in (2 * pair, 2 * pair + 1):
+        def quantise_r(pair, h):
+            codes = quant.tile([P, 512], U32, name="codes_r", align_bytes=64)
+            scales = quant.tile([P, 512], U8, name="scales_r", align_bytes=64)
+            nc.vector.quantize_mx(
+                out=codes[:].bitcast(E4X4),
+                scales=scales[:],
+                in_=state[(pair, "r", "wide")][:, 2048 * h : 2048 * (h + 1)],
+            )
+            state[(pair, h, "r")] = (codes, scales)
+
+        def quantise_g(pair, h, half):
+            if half == 0:
+                state[(pair, h, "g")] = (
+                    quant.tile([P, 512], U32, name="codes_g", align_bytes=64),
+                    quant.tile([P, 512], U8, name="scales_g", align_bytes=64),
+                )
+            codes, scales = state[(pair, h, "g")]
+            cols = slice(256 * half, 256 * (half + 1))
+            lo = 2048 * h + 1024 * half
+            nc.vector.quantize_mx(
+                out=codes[:, cols].bitcast(E5X4),
+                scales=scales[:, cols],
+                in_=state[(pair, "g", "wide")][:, lo : lo + 1024],
+            )
+
+        def multiply(pair, h, half):
+            r_codes, r_scales = state[(pair, h, "r")]
+            g_codes, g_scales = state[(pair, h, "g")]
+            if half == 0:
+                state[(pair, h, "res")] = results.tile(
+                    [P, 4 * N], FP32, name="res%d" % (2 * pair + h)
+                )
+            for m in (2 * half, 2 * half + 1):
                 acc = psum_o.tile([P, N], FP32, name="acc")
                 cols = slice(P * m, P * (m + 1))
                 nc.tensor.matmul_mx(
@@ -127,18 +127,15 @@ def tile_gcn_kernel(tc, regional_means, adj, grad_out, out):
                     start=True,
                     stop=True,
                 )
-                accs.append(acc)
-            state[(b, "acc", pair)] = accs
+                state[(pair, h, "acc", m)] = acc
 
-        def leave(b, pair):
-            if pair == 0:
-                state[(b, "res")] = results.tile([P, 4 * N], FP32, name="res%d" % b)
-            res = state[(b, "res")]
-            for i in range(2):
-                m = 2 * pair + i
+        def leave(pair, h, half):
+            res = state[(pair, h, "res")]
+            for m in (2 * half, 2 * half + 1):
                 cols = slice(N * m, N * (m + 1))
+                acc = state[(pair, h, "acc", m)]
                 if m == 1:
-                    nc.scalar.copy(out=res[:, cols], in_=state[(b, "acc", pair)][i][:])
+                    nc.scalar.copy(out=res[:, cols], in_=acc[:])
                     nc.gpsimd.affine_select(
                         out=res[:, cols],
                         in_=res[:, cols],
@@ -150,30 +147,44 @@ def tile_gcn_kernel(tc, regional_means, adj, grad_out, out):
                     )
                 else:
                     nc.vector.tensor_tensor(
-                        out=res[:, cols],
-                        in0=state[(b, "acc", pair)][i][:],
-                        in1=mask[:, cols],
-                        op=mybir.AluOpType.mult,
+                        out=res[:, cols], in0=acc[:], in1=mask[:, cols], op=mybir.AluOpType.mult
                     )
+            if half == 1:
+                nc.sync.dma_start(
+                    out=out[2 * pair + h].rearrange("(p m) j -> p (m j)", m=4), in_=res[:]
+                )
 
-        transposes(0, "r")
-        quantise(0, "r")
-        transposes(0, "g")
-        quantise(0, "g")
-        for b in range(B):
-            more = b + 1 < B
-            dst = out[b].rearrange("(p m) j -> p m j", m=4)
+        transposes(0, "r", 0)
+        transposes(0, "r", 1)
+        quantise_r(0, 0)
+        quantise_r(0, 1)
+        transposes(0, "g", 0)
+        quantise_g(0, 0, 0)
+        quantise_g(0, 1, 0)
+        transposes(0, "g", 1)
+        for pair in range(PAIRS):
+            more = pair + 1 < PAIRS
             if more:
-                transposes(b + 1, "r")
-            multiply(b, 0)
+                transposes(pair + 1, "r", 0)
+            multiply(pair, 0, 0)
+            quantise_g(pair, 0, 1)
+            quantise_g(pair, 1, 1)
+            leave(pair, 0, 0)
             if more:
-                quantise(b + 1, "r")
-            leave(b, 0)
+                transposes(pair + 1, "r", 1)
+            multiply(pair, 0, 1)
+            leave(pair, 0, 1)
             if more:
-                transposes(b + 1, "g")
-            multiply(b, 1)
+                transposes(pair + 1, "g", 0)
+            multiply(pair, 1, 0)
             if more:
-                quantise(b + 1, "g")
-            leave(b, 1)
-            src = state[(b, "res")][:].rearrange("p (m j) -> p m j", m=4)
-            nc.sync.dma_start(out=dst, in_=src)
+                quantise_r(pair + 1, 0)
+                quantise_r(pair + 1, 1)
+            leave(pair, 1, 0)
+            if more:
+                transposes(pair + 1, "g", 1)
+            multiply(pair, 1, 1)
+            if more:
+                quantise_g(pair + 1, 0, 0)
+                quantise_g(pair + 1, 1, 0)
+            leave(pair, 1, 1)

@@ -75,13 +75,11 @@ def tile_gcn_kernel(tc, regional_means, adj, grad_out, out):
                         bank[:, 128 * a : 128 * (a + 1)], words[:, lo : lo + 128], ident[:]
                     )
                 if which == "r":
-                    dst = wide_words.rearrange("p (h c i a) -> p i h c a", h=2, i=4, a=4)
+                    dst = wide_words.rearrange("p (h c i a) -> p i h c a", h=2, i=4, a=4)[:, i]
                 else:
-                    dst = wide_words.rearrange("p (h i c a) -> p i h c a", h=2, i=4, a=4)
-                nc.scalar.copy(
-                    out=dst[:, i],
-                    in_=bank[:].rearrange("p (a h c) -> p h c a", a=4, h=2),
-                )
+                    dst = wide_words.rearrange("p (f h e c a) -> p f e h c a", f=2, h=2, e=2, a=4)
+                    dst = dst[:, run, i % 2]
+                nc.scalar.copy(out=dst, in_=bank[:].rearrange("p (a h c) -> p h c a", a=4, h=2))
 
         def quantise_r(pair, h):
             codes = quant.tile([P, 512], U32, name="codes_r", align_bytes=64)
@@ -101,7 +99,7 @@ def tile_gcn_kernel(tc, regional_means, adj, grad_out, out):
                 )
             codes, scales = state[(pair, h, "g")]
             cols = slice(256 * half, 256 * (half + 1))
-            lo = 2048 * h + 1024 * half
+            lo = 2048 * half + 1024 * h
             nc.vector.quantize_mx(
                 out=codes[:, cols].bitcast(E5X4),
                 scales=scales[:, cols],

@@ -23,7 +23,6 @@ BYTES = 2 * (B * N * F * 2) + B * N * N * 4
 def tile_gcn_kernel(tc, regional_means, adj, grad_out, out):
     nc = tc.nc
     with ExitStack() as ctx:
-        ctx.enter_context(tc.manual_schedule())
         const = ctx.enter_context(tc.tile_pool(name="const", bufs=1))
         inputs = ctx.enter_context(tc.tile_pool(name="inputs", bufs=1))
         results = ctx.enter_context(tc.tile_pool(name="results", bufs=1))

from contextlib import ExitStack

import concourse.mybir as mybir
from concourse.masks import make_identity

FP32 = mybir.dt.float32
BF16 = mybir.dt.bfloat16
U32 = mybir.dt.uint32
U8 = mybir.dt.uint8
E4X4 = mybir.dt.float8_e4m3fn_x4
E5X4 = mybir.dt.float8_e5m2_x4

B = 8
N = 512
F = 512
P = 128
PAIRS = B // 2

FLOPS = 2 * B * N * N * F
BYTES = 2 * (B * N * F * 2) + B * N * N * 4


def tile_gcn_kernel(tc, regional_means, adj, grad_out, out):
    nc = tc.nc
    with ExitStack() as ctx:
        const = ctx.enter_context(tc.tile_pool(name="const", bufs=1))
        inputs = ctx.enter_context(tc.tile_pool(name="inputs", bufs=1))
        results = ctx.enter_context(tc.tile_pool(name="results", bufs=1))
        grouped = ctx.enter_context(tc.tile_pool(name="grouped", bufs=2))
        quant = ctx.enter_context(tc.tile_pool(name="quant", bufs=4))
        psum_t = ctx.enter_context(tc.psum_pool(name="psum_t", bufs=4))
        psum_o = ctx.enter_context(tc.psum_pool(name="psum_o", bufs=4))

        in_words = {}
        for pair in range(PAIRS):
            for which, src_all in (("r", regional_means), ("g", grad_out)):
                t = inputs.tile([P, 4096], BF16, name="%s_in%d" % (which, pair))
                rows = src_all.flatten_outer_dims()[2 * N * pair : 2 * N * (pair + 1), :]
                nc.sync.dma_start(out=t[:], in_=rows.rearrange("(p m) k -> p (m k)", m=8))
                in_words[(pair, which)] = t[:].bitcast(FP32)

        ident = const.tile([P, P], FP32, name="ident")
        make_identity(nc, ident[:])
        mask = const.tile([P, 4 * N], FP32, name="mask")
        nc.vector.memset(mask[:], 1.0)
        for m in range(4):
            nc.gpsimd.affine_select(
                out=mask[:, N * m : N * (m + 1)],
                in_=mask[:, N * m : N * (m + 1)],
                compare_op=mybir.AluOpType.not_equal,
                fill=0.0,
                base=m,
                pattern=[[-1, N]],
                channel_multiplier=4,
            )

        state = {}

        def transposes(pair, which, run):
            words = in_words[(pair, which)]
            if run == 0:
                state[(pair, which, "wide")] = grouped.tile(
                    [P, 4096], BF16, name="wide_" + which, align_bytes=64
                )
            wide_words = state[(pair, which, "wide")][:].bitcast(FP32)
            for i in (2 * run, 2 * run + 1):
                bank = psum_t.tile([P, 512], FP32, name="bank")
                for a in range(4):
                    if which == "r":
                        lo = 512 * i + 128 * a
                    else:
                        lo = 256 * (i + 4 * (a // 2)) + 128 * (a % 2)
                    nc.tensor.transpose(
                        bank[:, 128 * a : 128 * (a + 1)], words[:, lo : lo + 128], ident[:]
                    )
                if which == "r":
                    dst = wide_words.rearrange("p (h c i a) -> p i h c a", h=2, i=4, a=4)[:, i]
                else:
                    dst = wide_words.rearrange("p (f h e c a) -> p f e h c a", f=2, h=2, e=2, a=4)
                    dst = dst[:, run, i % 2]
                nc.scalar.copy(out=dst, in_=bank[:].rearrange("p (a h c) -> p h c a", a=4, h=2))

        def quantise_r(pair, h):
            codes = quant.tile([P, 512], U32, name="codes_r", align_bytes=64)
            scales = quant.tile([P, 512], U8, name="scales_r", align_bytes=64)
            nc.vector.quantize_mx(
                out=codes[:].bitcast(E4X4),
                scales=scales[:],
                in_=state[(pair, "r", "wide")][:, 2048 * h : 2048 * (h + 1)],
            )
            state[(pair, h, "r")] = (codes, scales)

        def quantise_g(pair, h, half):
            if half == 0:
                state[(pair, h, "g")] = (
                    quant.tile([P, 512], U32, name="codes_g", align_bytes=64),
                    quant.tile([P, 512], U8, name="scales_g", align_bytes=64),
                )
            codes, scales = state[(pair, h, "g")]
            cols = slice(256 * half, 256 * (half + 1))
            lo = 2048 * half + 1024 * h
            nc.vector.quantize_mx(
                out=codes[:, cols].bitcast(E5X4),
                scales=scales[:, cols],
                in_=state[(pair, "g", "wide")][:, lo : lo + 1024],
            )

        def multiply(pair, h, half):
            r_codes, r_scales = state[(pair, h, "r")]
            g_codes, g_scales = state[(pair, h, "g")]
            if half == 0:
                state[(pair, h, "res")] = results.tile(
                    [P, 4 * N], FP32, name="res%d" % (2 * pair + h)
                )
            for m in (2 * half, 2 * half + 1):
                acc = psum_o.tile([P, N], FP32, name="acc")
                cols = slice(P * m, P * (m + 1))
                nc.tensor.matmul_mx(
                    out=acc[:],
                    lhsT=g_codes[:, cols].bitcast(E5X4),
                    lhsT_scale=g_scales[:, cols],
                    rhs=r_codes[:].bitcast(E4X4),
                    rhs_scale=r_scales[:],
                    start=True,
                    stop=True,
                )
                state[(pair, h, "acc", m)] = acc

        def leave(pair, h, half):
            res = state[(pair, h, "res")]
            for m in (2 * half, 2 * half + 1):
                cols = slice(N * m, N * (m + 1))
                acc = state[(pair, h, "acc", m)]
                if m == 1:
                    nc.scalar.copy(out=res[:, cols], in_=acc[:])
                    nc.gpsimd.affine_select(
                        out=res[:, cols],
                        in_=res[:, cols],
                        compare_op=mybir.AluOpType.not_equal,
                        fill=0.0,
                        base=m,
                        pattern=[[-1, N]],
                        channel_multiplier=4,
                    )
                else:
                    nc.vector.tensor_tensor(
                        out=res[:, cols], in0=acc[:], in1=mask[:, cols], op=mybir.AluOpType.mult
                    )
            if half == 1:
                nc.sync.dma_start(
                    out=out[2 * pair + h].rearrange("(p m) j -> p (m j)", m=4), in_=res[:]
                )

        transposes(0, "r", 0)
        transposes(0, "r", 1)
        quantise_r(0, 0)
        quantise_r(0, 1)
        transposes(0, "g", 0)
        quantise_g(0, 0, 0)
        quantise_g(0, 1, 0)
        transposes(0, "g", 1)
        for pair in range(PAIRS):
            more = pair + 1 < PAIRS
            if more:
                transposes(pair + 1, "r", 0)
            multiply(pair, 0, 0)
            quantise_g(pair, 0, 1)
            quantise_g(pair, 1, 1)
            leave(pair, 0, 0)
            if more:
                transposes(pair + 1, "r", 1)
            multiply(pair, 0, 1)
            leave(pair, 0, 1)
            if more:
                transposes(pair + 1, "g", 0)
            multiply(pair, 1, 0)
            if more:
                quantise_r(pair + 1, 0)
                quantise_r(pair + 1, 1)
            leave(pair, 1, 0)
            if more:
                transposes(pair + 1, "g", 1)
            multiply(pair, 1, 1)
            if more:
                quantise_g(pair + 1, 0, 0)
                quantise_g(pair + 1, 1, 0)
            leave(pair, 1, 1)
